import numpy as np
import ml_dtypes


def mxq(x, axis, fmt="e4m3"):
    dtype, down = {"e4m3": (ml_dtypes.float8_e4m3fn, 7), "e5m2": (ml_dtypes.float8_e5m2, 14)}[fmt]
    v = np.moveaxis(np.asarray(x, np.float32).astype(ml_dtypes.bfloat16).astype(np.float64), axis, -1)
    blocks = v.reshape(v.shape[:-1] + (-1, 32))
    amax = np.abs(blocks).max(-1, keepdims=True)
    byte = np.maximum(np.where(amax > 0, np.frexp(amax)[1] - 1 + 127, 0) - down, 1)
    scale = np.exp2(byte - 127.0)
    codes = (blocks / scale).astype(np.float32).astype(dtype).astype(np.float64)
    return np.moveaxis((codes * scale).reshape(v.shape), -1, axis)


WIDE = False


def mx_kscale(k):
    if not WIDE:
        return np.ones(k)
    levels = np.array([10, -10, 5, -5, 0])
    a = np.random.permutation(np.resize(levels, k // 512 * 4)).reshape(k // 512, 4)
    idx = np.arange(k)
    return np.exp2(a[idx // 512, idx % 128 // 32])


BF16 = ml_dtypes.bfloat16


def bf(x):
    return np.asarray(x, np.float32).astype(BF16)


def f64(x):
    return np.asarray(x).astype(np.float64)


B, S, H, NH, NKV, HD = 2, 64, 512, 16, 4, 128
ROPE_THETA = 10000.0


def rope_tables():
    inv_freq = 1.0 / (ROPE_THETA ** (np.arange(0, HD, 2) / HD))
    pos = np.arange(S)[None, :] + np.random.randint(0, S, (B, 1))
    freqs = pos[:, :, None] * inv_freq[None, None, :]
    emb = np.concatenate([freqs, freqs], axis=-1)
    return np.cos(emb), np.sin(emb)


def rotate_half(x):
    x1, x2 = np.split(x, 2, axis=-1)
    return np.concatenate([-x2, x1], axis=-1)


def setup_inputs():
    s = mx_kscale(H)
    hidden_states = bf(np.random.standard_normal((B, S, H)) * s)
    q_w = bf(np.random.standard_normal((NH * HD, H)) / np.sqrt(H) / s[None, :])
    k_w = bf(np.random.standard_normal((NKV * HD, H)) / np.sqrt(H) / s[None, :])
    v_w = bf(np.random.standard_normal((NKV * HD, H)) / np.sqrt(H) / s[None, :])
    cos, sin = rope_tables()
    return {"hidden_states": hidden_states, "cos": bf(cos), "sin": bf(sin), "q_w": q_w, "k_w": k_w, "v_w": v_w}


def reference(hidden_states, cos, sin, q_w, k_w, v_w):
    b, s, _ = hidden_states.shape
    xq = mxq(f64(hidden_states), 2, "e4m3")
    q = (xq @ mxq(f64(q_w), 1, "e4m3").T).reshape(b, s, NH, HD).transpose(0, 2, 1, 3)
    k = (xq @ mxq(f64(k_w), 1, "e4m3").T).reshape(b, s, NKV, HD).transpose(0, 2, 1, 3)
    v = (xq @ mxq(f64(v_w), 1, "e4m3").T).reshape(b, s, NKV, HD).transpose(0, 2, 1, 3)
    c = f64(cos)[:, None, :, :]
    sn = f64(sin)[:, None, :, :]
    q = q * c + rotate_half(q) * sn
    k = k * c + rotate_half(k) * sn
    return (q, k, v)

@@ -1,0 +1,168 @@
+from contextlib import ExitStack
+
+import concourse.mybir as mybir
+from concourse.masks import make_identity
+
+BF16 = mybir.dt.bfloat16
+F32 = mybir.dt.float32
+U32 = mybir.dt.uint32
+U8 = mybir.dt.uint8
+FP8X4 = mybir.dt.float8_e4m3fn_x4
+MULT = mybir.AluOpType.mult
+ADD = mybir.AluOpType.add
+
+P = 128
+PACK = 4
+B, S, H = 2, 64, 512
+HD = 128
+HALF = HD // 2
+WORD_COLS = H // 2
+PLANES = WORD_COLS // P
+ROWS = 2
+UNIT = ROWS * P
+CHUNK = 512
+UNITS = CHUNK // UNIT
+HEADS = CHUNK // HD
+
+FLOPS = 2 * B * S * H * (2048 + 512 + 512)
+
+
+def transpose_words(nc, bank_rows, rows, ident):
+    words = rows.bitcast(F32)
+    for u in range(PLANES):
+        nc.tensor.transpose(bank_rows[:, u, :], words[:, u * P : (u + 1) * P], ident)
+
+
+def tile_mistralattention_s_kernel(
+    tc, hidden_states, cos, sin, q_w, k_w, v_w, q_out, k_out, v_out
+):
+    nc = tc.nc
+
+    chunks = []
+    for w, dst, rotary in ((q_w, q_out, True), (k_w, k_out, True), (v_w, v_out, False)):
+        for c in range(w.shape[0] // CHUNK):
+            rows = w[c * CHUNK : (c + 1) * CHUNK, :]
+            heads = dst[:, c * HEADS : (c + 1) * HEADS]
+            chunks.append((rows, heads, rotary))
+    n_chunks = len(chunks)
+
+    with ExitStack() as ctx:
+        keep = ctx.enter_context(tc.tile_pool(name="keep", bufs=1))
+        work = ctx.enter_context(tc.tile_pool(name="work", bufs=n_chunks))
+        tr_psum = ctx.enter_context(tc.psum_pool(name="tr_psum", bufs=4))
+        acc_psum = ctx.enter_context(tc.psum_pool(name="acc_psum", bufs=4))
+
+        x_sb = keep.tile([P, H], BF16)
+        cos_sb = keep.tile([P, HD], BF16)
+        sin_sb = keep.tile([P, HD], BF16)
+        for b in range(B):
+            nc.sync.dma_start(out=x_sb[b:P:B, :], in_=hidden_states[b])
+        w_sb = []
+        for c in range(n_chunks):
+            w_chunk = keep.tile([P, UNITS, ROWS, H], BF16, name="w%d" % c)
+            w_sb.append(w_chunk)
+            for g in range(UNITS):
+                unit_rows = chunks[c][0][g * UNIT : (g + 1) * UNIT, :]
+                nc.sync.dma_start(
+                    out=w_chunk[:, g], in_=unit_rows.rearrange("(p r) k -> p r k", r=ROWS)
+                )
+            if c == 0:
+                for b in range(B):
+                    nc.sync.dma_start(out=cos_sb[b:P:B, :], in_=cos[b])
+                    nc.sync.dma_start(out=sin_sb[b:P:B, :], in_=sin[b])
+
+        ident = keep.tile([P, P], F32)
+        make_identity(nc, ident[:])
+
+        x_bank = tr_psum.tile([P, ROWS, PLANES, P], F32, name="bank")
+        transpose_words(nc, x_bank[:, 0], x_sb[:], ident[:])
+        x_grouped = keep.tile([P, P * PACK], BF16, align_bytes=64)
+        nc.scalar.copy(
+            out=x_grouped[:].bitcast(F32).rearrange("p (n u) -> p n u", u=PLANES),
+            in_=x_bank[:, 0].rearrange("p u n -> p n u"),
+        )
+        x_codes = keep.tile([P, P], U32, align_bytes=64)
+        x_scales = keep.tile([P, P], U8, align_bytes=64)
+        nc.vector.quantize_mx(
+            out=x_codes[:].bitcast(FP8X4), scales=x_scales[:], in_=x_grouped[:]
+        )
+
+        nc.vector.tensor_scalar_mul(sin_sb[:, 0:HALF], sin_sb[:, 0:HALF], -1.0)
+
+        grouped = {}
+        codes = {}
+        scales = {}
+        acc = {}
+
+        def regroup(c):
+            grouped[c] = work.tile([P, CHUNK * PACK], BF16, name="grouped", align_bytes=64)
+            grouped_words = grouped[c][:].bitcast(F32)
+            for g in range(UNITS):
+                bank = tr_psum.tile([P, ROWS, PLANES, P], F32, name="bank")
+                for r in range(ROWS):
+                    transpose_words(nc, bank[:, r], w_sb[c][:, g, r, :], ident[:])
+                unit_words = grouped_words[:, g * UNIT * PLANES : (g + 1) * UNIT * PLANES]
+                nc.scalar.copy(
+                    out=unit_words.rearrange("p (n r u) -> p n r u", r=ROWS, u=PLANES),
+                    in_=bank[:].rearrange("p r u n -> p n r u"),
+                )
+
+        def project(c):
+            codes[c] = work.tile([P, CHUNK], U32, name="codes", align_bytes=64)
+            scales[c] = work.tile([P, CHUNK], U8, name="scales", align_bytes=64)
+            nc.vector.quantize_mx(
+                out=codes[c][:].bitcast(FP8X4), scales=scales[c][:], in_=grouped[c][:]
+            )
+            acc[c] = acc_psum.tile([P, CHUNK], F32, name="acc")
+            nc.tensor.matmul_mx(
+                out=acc[c][:],
+                lhsT=x_codes[:].bitcast(FP8X4),
+                lhsT_scale=x_scales[:],
+                rhs=codes[c][:].bitcast(FP8X4),
+                rhs_scale=scales[c][:],
+                start=True,
+                stop=True,
+            )
+
+        def finish(c):
+            result = work.tile([P, CHUNK], F32, name="result")
+            if chunks[c][2]:
+                straight = work.tile([P, HEADS, HD], F32, name="straight")
+                crossed = work.tile([P, HEADS, 2, HALF], F32, name="crossed")
+                nc.vector.tensor_tensor(
+                    out=straight[:],
+                    in0=acc[c][:].rearrange("p (h d) -> p h d", d=HD),
+                    in1=cos_sb[:].unsqueeze(1).to_broadcast([P, HEADS, HD]),
+                    op=MULT,
+                )
+                halves = acc[c][:].rearrange("p (h f j) -> p h f j", f=2, j=HALF)
+                for f in range(2):
+                    nc.vector.tensor_tensor(
+                        out=crossed[:, :, f, :],
+                        in0=halves[:, :, 1 - f, :],
+                        in1=sin_sb[:, f * HALF : (f + 1) * HALF]
+                        .unsqueeze(1)
+                        .to_broadcast([P, HEADS, HALF]),
+                        op=MULT,
+                    )
+                nc.vector.tensor_tensor(
+                    out=result[:],
+                    in0=straight[:].rearrange("p h d -> p (h d)"),
+                    in1=crossed[:].rearrange("p h f j -> p (h f j)"),
+                    op=ADD,
+                )
+            else:
+                nc.scalar.copy(out=result[:], in_=acc[c][:])
+            for b in range(B):
+                nc.sync.dma_start(
+                    out=chunks[c][1][b].rearrange("h s d -> s h d"),
+                    in_=result[b:P:B, :].rearrange("p (h d) -> p h d", d=HD),
+                )
+
+        for step in range(n_chunks + 2):
+            if step < n_chunks:
+                regroup(step)
+            if 1 <= step <= n_chunks:
+                project(step - 1)
+            if step >= 2:
+                finish(step - 2)

@@ -136,16 +136,16 @@ def tile_mistralattention_s_kernel(
                     op=MULT,
                 )
                 halves = acc[c][:].rearrange("p (h f j) -> p h f j", f=2, j=HALF)
-                for f in range(2):
-                    nc.vector.tensor_tensor(
-                        out=crossed[:, :, f, :],
-                        in0=halves[:, :, 1 - f, :],
-                        in1=sin_sb[:, f * HALF : (f + 1) * HALF]
-                        .unsqueeze(1)
-                        .to_broadcast([P, HEADS, HALF]),
-                        op=MULT,
-                    )
                 nc.vector.tensor_tensor(
+                    out=crossed[:],
+                    in0=halves[:, :, ::-1, :],
+                    in1=sin_sb[:]
+                    .rearrange("p (f j) -> p f j", j=HALF)
+                    .unsqueeze(1)
+                    .to_broadcast([P, HEADS, 2, HALF]),
+                    op=MULT,
+                )
+                nc.gpsimd.tensor_tensor(
                     out=result[:],
                     in0=straight[:].rearrange("p h d -> p (h d)"),
                     in1=crossed[:].rearrange("p h f j -> p (h f j)"),

@@ -23,6 +23,7 @@ UNIT = ROWS * P
 CHUNK = 512
 UNITS = CHUNK // UNIT
 HEADS = CHUNK // HD
+ISSUES = 2
 
 FLOPS = 2 * B * S * H * (2048 + 512 + 512)
 
@@ -45,6 +46,7 @@ def tile_mistralattention_s_kernel(
             heads = dst[:, c * HEADS : (c + 1) * HEADS]
             chunks.append((rows, heads, rotary))
     n_chunks = len(chunks)
+    last_rotary = max(c for c in range(n_chunks) if chunks[c][2])
 
     with ExitStack() as ctx:
         keep = ctx.enter_context(tc.tile_pool(name="keep", bufs=1))
@@ -114,15 +116,16 @@ def tile_mistralattention_s_kernel(
                 out=codes[c][:].bitcast(FP8X4), scales=scales[c][:], in_=grouped[c][:]
             )
             acc[c] = acc_psum.tile([P, CHUNK], F32, name="acc")
-            nc.tensor.matmul_mx(
-                out=acc[c][:],
-                lhsT=x_codes[:].bitcast(FP8X4),
-                lhsT_scale=x_scales[:],
-                rhs=codes[c][:].bitcast(FP8X4),
-                rhs_scale=scales[c][:],
-                start=True,
-                stop=True,
-            )
+            for issue in range(ISSUES):
+                nc.tensor.matmul_mx(
+                    out=acc[c][:],
+                    lhsT=x_codes[:].bitcast(FP8X4),
+                    lhsT_scale=x_scales[:],
+                    rhs=codes[c][:].bitcast(FP8X4),
+                    rhs_scale=scales[c][:],
+                    start=True,
+                    stop=True,
+                )
 
         def finish(c):
             result = work.tile([P, CHUNK], F32, name="result")
@@ -145,7 +148,8 @@ def tile_mistralattention_s_kernel(
                     .to_broadcast([P, HEADS, 2, HALF]),
                     op=MULT,
                 )
-                nc.gpsimd.tensor_tensor(
+                adder = nc.vector if c == last_rotary else nc.gpsimd
+                adder.tensor_tensor(
                     out=result[:],
                     in0=straight[:].rearrange("p h d -> p (h d)"),
                     in1=crossed[:].rearrange("p h f j -> p (h f j)"),

@@ -21,9 +21,7 @@ PLANES = WORD_COLS // P
 ROWS = 2
 UNIT = ROWS * P
 CHUNK = 512
-UNITS = CHUNK // UNIT
-HEADS = CHUNK // HD
-ISSUES = 2
+HEAD_PIECES = (UNIT, UNIT)
 
 FLOPS = 2 * B * S * H * (2048 + 512 + 512)
 
@@ -39,134 +37,194 @@ def tile_mistralattention_s_kernel(
 ):
     nc = tc.nc
 
-    chunks = []
+    pieces = []
     for w, dst, rotary in ((q_w, q_out, True), (k_w, k_out, True), (v_w, v_out, False)):
-        for c in range(w.shape[0] // CHUNK):
-            rows = w[c * CHUNK : (c + 1) * CHUNK, :]
-            heads = dst[:, c * HEADS : (c + 1) * HEADS]
-            chunks.append((rows, heads, rotary))
-    n_chunks = len(chunks)
-    last_rotary = max(c for c in range(n_chunks) if chunks[c][2])
+        row = 0
+        while row < w.shape[0]:
+            n_rows = HEAD_PIECES[len(pieces)] if len(pieces) < len(HEAD_PIECES) else CHUNK
+            pieces.append(
+                (w[row : row + n_rows, :], dst[:, row // HD : (row + n_rows) // HD], rotary, n_rows)
+            )
+            row += n_rows
+    n_pieces = len(pieces)
+    n_head = len(HEAD_PIECES)
+    last_rotary = max(i for i in range(n_pieces) if pieces[i][2])
 
     with ExitStack() as ctx:
         keep = ctx.enter_context(tc.tile_pool(name="keep", bufs=1))
-        work = ctx.enter_context(tc.tile_pool(name="work", bufs=n_chunks))
+        work = ctx.enter_context(tc.tile_pool(name="work", bufs=n_pieces + 1))
         tr_psum = ctx.enter_context(tc.psum_pool(name="tr_psum", bufs=4))
-        acc_psum = ctx.enter_context(tc.psum_pool(name="acc_psum", bufs=4))
+        acc_psum = ctx.enter_context(tc.psum_pool(name="acc_psum", bufs=3))
+        idle_psum = ctx.enter_context(tc.psum_pool(name="idle_psum", bufs=1))
+        ctx.enter_context(tc.manual_schedule())
 
         x_sb = keep.tile([P, H], BF16)
-        cos_sb = keep.tile([P, HD], BF16)
-        sin_sb = keep.tile([P, HD], BF16)
-        for b in range(B):
-            nc.sync.dma_start(out=x_sb[b:P:B, :], in_=hidden_states[b])
-        w_sb = []
-        for c in range(n_chunks):
-            w_chunk = keep.tile([P, UNITS, ROWS, H], BF16, name="w%d" % c)
-            w_sb.append(w_chunk)
-            for g in range(UNITS):
-                unit_rows = chunks[c][0][g * UNIT : (g + 1) * UNIT, :]
+        tables = keep.tile([P, 2, HD], BF16)
+        w_units = [[] for i in range(n_pieces)]
+
+        def load(i):
+            for row in range(0, pieces[i][3], UNIT):
+                unit = keep.tile([P, ROWS, H], BF16, name="w%d_%d" % (i, row))
                 nc.sync.dma_start(
-                    out=w_chunk[:, g], in_=unit_rows.rearrange("(p r) k -> p r k", r=ROWS)
+                    out=unit[:],
+                    in_=pieces[i][0][row : row + UNIT, :].rearrange("(p r) k -> p r k", r=ROWS),
                 )
-            if c == 0:
-                for b in range(B):
-                    nc.sync.dma_start(out=cos_sb[b:P:B, :], in_=cos[b])
-                    nc.sync.dma_start(out=sin_sb[b:P:B, :], in_=sin[b])
+                w_units[i].append(unit)
+
+        load(0)
+        nc.sync.dma_start(out=x_sb[:], in_=hidden_states.flatten_outer_dims())
+        load(1)
+        nc.sync.dma_start(out=tables[:, 0, :], in_=cos.flatten_outer_dims())
+        nc.sync.dma_start(out=tables[:, 1, :], in_=sin.flatten_outer_dims())
+        for i in range(2, n_pieces):
+            load(i)
 
         ident = keep.tile([P, P], F32)
         make_identity(nc, ident[:])
-
-        x_bank = tr_psum.tile([P, ROWS, PLANES, P], F32, name="bank")
-        transpose_words(nc, x_bank[:, 0], x_sb[:], ident[:])
-        x_grouped = keep.tile([P, P * PACK], BF16, align_bytes=64)
-        nc.scalar.copy(
-            out=x_grouped[:].bitcast(F32).rearrange("p (n u) -> p n u", u=PLANES),
-            in_=x_bank[:, 0].rearrange("p u n -> p n u"),
+        shuffle = keep.tile([P, P], BF16)
+        nc.vector.tensor_copy(
+            out=shuffle[:].rearrange("p (s b) -> p s b", b=B),
+            in_=ident[:].rearrange("p (b s) -> p s b", b=B),
         )
+
         x_codes = keep.tile([P, P], U32, align_bytes=64)
         x_scales = keep.tile([P, P], U8, align_bytes=64)
-        nc.vector.quantize_mx(
-            out=x_codes[:].bitcast(FP8X4), scales=x_scales[:], in_=x_grouped[:]
-        )
-
-        nc.vector.tensor_scalar_mul(sin_sb[:, 0:HALF], sin_sb[:, 0:HALF], -1.0)
-
+        trig = keep.tile([P, 2, HD], BF16)
         grouped = {}
         codes = {}
         scales = {}
         acc = {}
 
-        def regroup(c):
-            grouped[c] = work.tile([P, CHUNK * PACK], BF16, name="grouped", align_bytes=64)
-            grouped_words = grouped[c][:].bitcast(F32)
-            for g in range(UNITS):
+        def prepare_x():
+            x_bank = tr_psum.tile([P, PLANES, P], F32, name="bank")
+            transpose_words(nc, x_bank[:], x_sb[:], ident[:])
+            x_grouped = keep.tile([P, P * PACK], BF16, align_bytes=64)
+            nc.vector.tensor_copy(
+                out=x_grouped[:].bitcast(F32).rearrange("p (s b u) -> p s b u", b=B, u=PLANES),
+                in_=x_bank[:].rearrange("p u (b s) -> p s b u", b=B),
+            )
+            nc.vector.quantize_mx(
+                out=x_codes[:].bitcast(FP8X4), scales=x_scales[:], in_=x_grouped[:]
+            )
+
+        def shuffle_tables():
+            bank = tr_psum.tile([P, 2, HD], F32, name="bank")
+            nc.tensor.matmul(
+                bank[:].rearrange("p t d -> p (t d)"),
+                lhsT=shuffle[:],
+                rhs=tables[:].rearrange("p t d -> p (t d)"),
+                start=True,
+                stop=True,
+            )
+            nc.vector.tensor_copy(out=trig[:], in_=bank[:])
+            nc.gpsimd.tensor_scalar_mul(trig[:, 1, 0:HALF], trig[:, 1, 0:HALF], -1.0)
+
+        def regroup(i, units=None):
+            if i not in grouped:
+                grouped[i] = work.tile(
+                    [P, pieces[i][3] * PACK], BF16, name="grouped", align_bytes=64
+                )
+            for j in units if units is not None else range(len(w_units[i])):
                 bank = tr_psum.tile([P, ROWS, PLANES, P], F32, name="bank")
                 for r in range(ROWS):
-                    transpose_words(nc, bank[:, r], w_sb[c][:, g, r, :], ident[:])
-                unit_words = grouped_words[:, g * UNIT * PLANES : (g + 1) * UNIT * PLANES]
+                    transpose_words(nc, bank[:, r], w_units[i][j][:, r, :], ident[:])
                 nc.scalar.copy(
-                    out=unit_words.rearrange("p (n r u) -> p n r u", r=ROWS, u=PLANES),
+                    out=grouped[i][:]
+                    .bitcast(F32)[:, j * UNIT * PLANES : (j + 1) * UNIT * PLANES]
+                    .rearrange("p (n r u) -> p n r u", r=ROWS, u=PLANES),
                     in_=bank[:].rearrange("p r u n -> p n r u"),
                 )
 
-        def project(c):
-            codes[c] = work.tile([P, CHUNK], U32, name="codes", align_bytes=64)
-            scales[c] = work.tile([P, CHUNK], U8, name="scales", align_bytes=64)
+        def quantise(i):
+            n_rows = pieces[i][3]
+            codes[i] = work.tile([P, n_rows], U32, name="codes", align_bytes=64)
+            scales[i] = work.tile([P, n_rows], U8, name="scales", align_bytes=64)
             nc.vector.quantize_mx(
-                out=codes[c][:].bitcast(FP8X4), scales=scales[c][:], in_=grouped[c][:]
+                out=codes[i][:].bitcast(FP8X4), scales=scales[i][:], in_=grouped[i][:]
             )
-            acc[c] = acc_psum.tile([P, CHUNK], F32, name="acc")
-            for issue in range(ISSUES):
+
+        def multiply(i):
+            acc[i] = acc_psum.tile([P, pieces[i][3]], F32, name="acc")
+            outs = [acc[i]]
+            if n_head <= i < n_pieces - 2:
+                idle = idle_psum.tile([P, pieces[i][3]], F32, name="idle")
+                outs.append(idle)
+            for out in outs:
                 nc.tensor.matmul_mx(
-                    out=acc[c][:],
+                    out=out[:],
                     lhsT=x_codes[:].bitcast(FP8X4),
                     lhsT_scale=x_scales[:],
-                    rhs=codes[c][:].bitcast(FP8X4),
-                    rhs_scale=scales[c][:],
+                    rhs=codes[i][:].bitcast(FP8X4),
+                    rhs_scale=scales[i][:],
                     start=True,
                     stop=True,
                 )
 
-        def finish(c):
-            result = work.tile([P, CHUNK], F32, name="result")
-            if chunks[c][2]:
-                straight = work.tile([P, HEADS, HD], F32, name="straight")
-                crossed = work.tile([P, HEADS, 2, HALF], F32, name="crossed")
-                nc.vector.tensor_tensor(
-                    out=straight[:],
-                    in0=acc[c][:].rearrange("p (h d) -> p h d", d=HD),
-                    in1=cos_sb[:].unsqueeze(1).to_broadcast([P, HEADS, HD]),
-                    op=MULT,
-                )
-                halves = acc[c][:].rearrange("p (h f j) -> p h f j", f=2, j=HALF)
-                nc.vector.tensor_tensor(
-                    out=crossed[:],
-                    in0=halves[:, :, ::-1, :],
-                    in1=sin_sb[:]
-                    .rearrange("p (f j) -> p f j", j=HALF)
-                    .unsqueeze(1)
-                    .to_broadcast([P, HEADS, 2, HALF]),
-                    op=MULT,
-                )
-                adder = nc.vector if c == last_rotary else nc.gpsimd
-                adder.tensor_tensor(
-                    out=result[:],
-                    in0=straight[:].rearrange("p h d -> p (h d)"),
-                    in1=crossed[:].rearrange("p h f j -> p (h f j)"),
-                    op=ADD,
-                )
-            else:
-                nc.scalar.copy(out=result[:], in_=acc[c][:])
+        def store(queue, i, first, heads, result):
             for b in range(B):
-                nc.sync.dma_start(
-                    out=chunks[c][1][b].rearrange("h s d -> s h d"),
+                queue.dma_start(
+                    out=pieces[i][1][b, first : first + heads].rearrange("h s d -> s h d"),
                     in_=result[b:P:B, :].rearrange("p (h d) -> p h d", d=HD),
                 )
 
-        for step in range(n_chunks + 2):
-            if step < n_chunks:
-                regroup(step)
-            if 1 <= step <= n_chunks:
-                project(step - 1)
-            if step >= 2:
-                finish(step - 2)
+        def rotate(i, first, heads, adder):
+            sums = acc[i][:, first * HD : (first + heads) * HD]
+            straight = work.tile([P, heads, HD], F32, name="straight")
+            crossed = work.tile([P, heads, 2, HALF], F32, name="crossed")
+            result = work.tile([P, heads * HD], F32, name="result")
+            nc.vector.tensor_tensor(
+                out=straight[:],
+                in0=sums.rearrange("p (h d) -> p h d", d=HD),
+                in1=trig[:, 0, :].unsqueeze(1).to_broadcast([P, heads, HD]),
+                op=MULT,
+            )
+            nc.vector.tensor_tensor(
+                out=crossed[:],
+                in0=sums.rearrange("p (h f j) -> p h f j", f=2, j=HALF)[:, :, ::-1, :],
+                in1=trig[:, 1, :]
+                .rearrange("p (f j) -> p f j", j=HALF)
+                .unsqueeze(1)
+                .to_broadcast([P, heads, 2, HALF]),
+                op=MULT,
+            )
+            adder.tensor_tensor(
+                out=result[:],
+                in0=straight[:].rearrange("p h d -> p (h d)"),
+                in1=crossed[:].rearrange("p h f j -> p (h f j)"),
+                op=ADD,
+            )
+            store(nc.sync, i, first, heads, result)
+
+        def finish(i):
+            heads = pieces[i][3] // HD
+            if not pieces[i][2]:
+                result = work.tile([P, heads * HD], F32, name="result")
+                nc.scalar.copy(out=result[:], in_=acc[i][:])
+                store(nc.scalar, i, 0, heads, result)
+            elif i < last_rotary:
+                rotate(i, 0, heads, nc.gpsimd)
+            else:
+                rotate(i, 0, heads // 2, nc.gpsimd)
+                rotate(i, heads // 2, heads - heads // 2, nc.vector)
+
+        regroup(0)
+        prepare_x()
+        quantise(0)
+        regroup(1)
+        shuffle_tables()
+        multiply(0)
+        quantise(1)
+        regroup(2, [0])
+        multiply(1)
+        regroup(2, [1])
+        finish(0)
+        finish(1)
+        regroup(3)
+        quantise(2)
+        for i in range(n_head, n_pieces):
+            if i + 2 < n_pieces:
+                regroup(i + 2)
+            multiply(i)
+            if i + 1 < n_pieces:
+                quantise(i + 1)
+            finish(i)

@@ -79,6 +79,11 @@ def tile_mistralattention_s_kernel(
         for i in range(2, n_pieces):
             load(i)
 
+        zeros = keep.tile([P, CHUNK], F32)
+        nc.vector.memset(zeros[:], 0.0)
+        warm = idle_psum.tile([P, CHUNK], F32, name="idle")
+        nc.tensor.matmul(warm[:], lhsT=zeros[:, 0:P], rhs=zeros[:], start=True, stop=True)
+
         ident = keep.tile([P, P], F32)
         make_identity(nc, ident[:])
         shuffle = keep.tile([P, P], BF16)

@@ -23,6 +23,8 @@ UNIT = ROWS * P
 CHUNK = 512
 HEAD_PIECES = (UNIT, UNIT)
 
+WARM_UP = 4
+
 FLOPS = 2 * B * S * H * (2048 + 512 + 512)
 
 
@@ -79,10 +81,11 @@ def tile_mistralattention_s_kernel(
         for i in range(2, n_pieces):
             load(i)
 
-        zeros = keep.tile([P, CHUNK], F32)
-        nc.vector.memset(zeros[:], 0.0)
+        zeros = keep.tile([P, P], F32)
+        nc.gpsimd.memset(zeros[:], 0.0)
         warm = idle_psum.tile([P, CHUNK], F32, name="idle")
-        nc.tensor.matmul(warm[:], lhsT=zeros[:, 0:P], rhs=zeros[:], start=True, stop=True)
+        for n in range(WARM_UP):
+            nc.tensor.matmul(warm[:, 0:P], lhsT=zeros[:], rhs=zeros[:], start=True, stop=True)
 
         ident = keep.tile([P, P], F32)
         make_identity(nc, ident[:])
@@ -113,6 +116,7 @@ def tile_mistralattention_s_kernel(
             )
 
         def shuffle_tables():
+            nc.gpsimd.tensor_scalar_mul(tables[:, 1, 0:HALF], tables[:, 1, 0:HALF], -1.0)
             bank = tr_psum.tile([P, 2, HD], F32, name="bank")
             nc.tensor.matmul(
                 bank[:].rearrange("p t d -> p (t d)"),
@@ -122,7 +126,6 @@ def tile_mistralattention_s_kernel(
                 stop=True,
             )
             nc.vector.tensor_copy(out=trig[:], in_=bank[:])
-            nc.gpsimd.tensor_scalar_mul(trig[:, 1, 0:HALF], trig[:, 1, 0:HALF], -1.0)
 
         def regroup(i, units=None):
             if i not in grouped:
@@ -151,9 +154,6 @@ def tile_mistralattention_s_kernel(
         def multiply(i):
             acc[i] = acc_psum.tile([P, pieces[i][3]], F32, name="acc")
             outs = [acc[i]]
-            if n_head <= i < n_pieces - 2:
-                idle = idle_psum.tile([P, pieces[i][3]], F32, name="idle")
-                outs.append(idle)
             for out in outs:
                 nc.tensor.matmul_mx(
                     out=out[:],
@@ -217,11 +217,11 @@ def tile_mistralattention_s_kernel(
         quantise(0)
         regroup(1)
         shuffle_tables()
+        regroup(2, [0])
         multiply(0)
         quantise(1)
-        regroup(2, [0])
-        multiply(1)
         regroup(2, [1])
+        multiply(1)
         finish(0)
         finish(1)
         regroup(3)

@@ -154,6 +154,9 @@ def tile_mistralattention_s_kernel(
         def multiply(i):
             acc[i] = acc_psum.tile([P, pieces[i][3]], F32, name="acc")
             outs = [acc[i]]
+            if n_head <= i < n_pieces - 2:
+                idle = idle_psum.tile([P, pieces[i][3]], F32, name="idle")
+                outs.append(idle)
             for out in outs:
                 nc.tensor.matmul_mx(
                     out=out[:],

from contextlib import ExitStack

import concourse.mybir as mybir
from concourse.masks import make_identity

BF16 = mybir.dt.bfloat16
F32 = mybir.dt.float32
U32 = mybir.dt.uint32
U8 = mybir.dt.uint8
FP8X4 = mybir.dt.float8_e4m3fn_x4
MULT = mybir.AluOpType.mult
ADD = mybir.AluOpType.add

P = 128
PACK = 4
B, S, H = 2, 64, 512
HD = 128
HALF = HD // 2
WORD_COLS = H // 2
PLANES = WORD_COLS // P
ROWS = 2
UNIT = ROWS * P
CHUNK = 512
HEAD_PIECES = (UNIT, UNIT)

WARM_UP = 4

FLOPS = 2 * B * S * H * (2048 + 512 + 512)


def transpose_words(nc, bank_rows, rows, ident):
    words = rows.bitcast(F32)
    for u in range(PLANES):
        nc.tensor.transpose(bank_rows[:, u, :], words[:, u * P : (u + 1) * P], ident)


def tile_mistralattention_s_kernel(
    tc, hidden_states, cos, sin, q_w, k_w, v_w, q_out, k_out, v_out
):
    nc = tc.nc

    pieces = []
    for w, dst, rotary in ((q_w, q_out, True), (k_w, k_out, True), (v_w, v_out, False)):
        row = 0
        while row < w.shape[0]:
            n_rows = HEAD_PIECES[len(pieces)] if len(pieces) < len(HEAD_PIECES) else CHUNK
            pieces.append(
                (w[row : row + n_rows, :], dst[:, row // HD : (row + n_rows) // HD], rotary, n_rows)
            )
            row += n_rows
    n_pieces = len(pieces)
    n_head = len(HEAD_PIECES)
    last_rotary = max(i for i in range(n_pieces) if pieces[i][2])

    with ExitStack() as ctx:
        keep = ctx.enter_context(tc.tile_pool(name="keep", bufs=1))
        work = ctx.enter_context(tc.tile_pool(name="work", bufs=n_pieces + 1))
        tr_psum = ctx.enter_context(tc.psum_pool(name="tr_psum", bufs=4))
        acc_psum = ctx.enter_context(tc.psum_pool(name="acc_psum", bufs=3))
        idle_psum = ctx.enter_context(tc.psum_pool(name="idle_psum", bufs=1))
        ctx.enter_context(tc.manual_schedule())

        x_sb = keep.tile([P, H], BF16)
        tables = keep.tile([P, 2, HD], BF16)
        w_units = [[] for i in range(n_pieces)]

        def load(i):
            for row in range(0, pieces[i][3], UNIT):
                unit = keep.tile([P, ROWS, H], BF16, name="w%d_%d" % (i, row))
                nc.sync.dma_start(
                    out=unit[:],
                    in_=pieces[i][0][row : row + UNIT, :].rearrange("(p r) k -> p r k", r=ROWS),
                )
                w_units[i].append(unit)

        load(0)
        nc.sync.dma_start(out=x_sb[:], in_=hidden_states.flatten_outer_dims())
        load(1)
        nc.sync.dma_start(out=tables[:, 0, :], in_=cos.flatten_outer_dims())
        nc.sync.dma_start(out=tables[:, 1, :], in_=sin.flatten_outer_dims())
        for i in range(2, n_pieces):
            load(i)

        zeros = keep.tile([P, P], F32)
        nc.gpsimd.memset(zeros[:], 0.0)
        warm = idle_psum.tile([P, CHUNK], F32, name="idle")
        for n in range(WARM_UP):
            nc.tensor.matmul(warm[:, 0:P], lhsT=zeros[:], rhs=zeros[:], start=True, stop=True)

        ident = keep.tile([P, P], F32)
        make_identity(nc, ident[:])
        shuffle = keep.tile([P, P], BF16)
        nc.vector.tensor_copy(
            out=shuffle[:].rearrange("p (s b) -> p s b", b=B),
            in_=ident[:].rearrange("p (b s) -> p s b", b=B),
        )

        x_codes = keep.tile([P, P], U32, align_bytes=64)
        x_scales = keep.tile([P, P], U8, align_bytes=64)
        trig = keep.tile([P, 2, HD], BF16)
        grouped = {}
        codes = {}
        scales = {}
        acc = {}

        def prepare_x():
            x_bank = tr_psum.tile([P, PLANES, P], F32, name="bank")
            transpose_words(nc, x_bank[:], x_sb[:], ident[:])
            x_grouped = keep.tile([P, P * PACK], BF16, align_bytes=64)
            nc.vector.tensor_copy(
                out=x_grouped[:].bitcast(F32).rearrange("p (s b u) -> p s b u", b=B, u=PLANES),
                in_=x_bank[:].rearrange("p u (b s) -> p s b u", b=B),
            )
            nc.vector.quantize_mx(
                out=x_codes[:].bitcast(FP8X4), scales=x_scales[:], in_=x_grouped[:]
            )

        def shuffle_tables():
            nc.gpsimd.tensor_scalar_mul(tables[:, 1, 0:HALF], tables[:, 1, 0:HALF], -1.0)
            bank = tr_psum.tile([P, 2, HD], F32, name="bank")
            nc.tensor.matmul(
                bank[:].rearrange("p t d -> p (t d)"),
                lhsT=shuffle[:],
                rhs=tables[:].rearrange("p t d -> p (t d)"),
                start=True,
                stop=True,
            )
            nc.vector.tensor_copy(out=trig[:], in_=bank[:])

        def regroup(i, units=None):
            if i not in grouped:
                grouped[i] = work.tile(
                    [P, pieces[i][3] * PACK], BF16, name="grouped", align_bytes=64
                )
            for j in units if units is not None else range(len(w_units[i])):
                bank = tr_psum.tile([P, ROWS, PLANES, P], F32, name="bank")
                for r in range(ROWS):
                    transpose_words(nc, bank[:, r], w_units[i][j][:, r, :], ident[:])
                nc.scalar.copy(
                    out=grouped[i][:]
                    .bitcast(F32)[:, j * UNIT * PLANES : (j + 1) * UNIT * PLANES]
                    .rearrange("p (n r u) -> p n r u", r=ROWS, u=PLANES),
                    in_=bank[:].rearrange("p r u n -> p n r u"),
                )

        def quantise(i):
            n_rows = pieces[i][3]
            codes[i] = work.tile([P, n_rows], U32, name="codes", align_bytes=64)
            scales[i] = work.tile([P, n_rows], U8, name="scales", align_bytes=64)
            nc.vector.quantize_mx(
                out=codes[i][:].bitcast(FP8X4), scales=scales[i][:], in_=grouped[i][:]
            )

        def multiply(i):
            acc[i] = acc_psum.tile([P, pieces[i][3]], F32, name="acc")
            outs = [acc[i]]
            if n_head <= i < n_pieces - 2:
                idle = idle_psum.tile([P, pieces[i][3]], F32, name="idle")
                outs.append(idle)
            for out in outs:
                nc.tensor.matmul_mx(
                    out=out[:],
                    lhsT=x_codes[:].bitcast(FP8X4),
                    lhsT_scale=x_scales[:],
                    rhs=codes[i][:].bitcast(FP8X4),
                    rhs_scale=scales[i][:],
                    start=True,
                    stop=True,
                )

        def store(queue, i, first, heads, result):
            for b in range(B):
                queue.dma_start(
                    out=pieces[i][1][b, first : first + heads].rearrange("h s d -> s h d"),
                    in_=result[b:P:B, :].rearrange("p (h d) -> p h d", d=HD),
                )

        def rotate(i, first, heads, adder):
            sums = acc[i][:, first * HD : (first + heads) * HD]
            straight = work.tile([P, heads, HD], F32, name="straight")
            crossed = work.tile([P, heads, 2, HALF], F32, name="crossed")
            result = work.tile([P, heads * HD], F32, name="result")
            nc.vector.tensor_tensor(
                out=straight[:],
                in0=sums.rearrange("p (h d) -> p h d", d=HD),
                in1=trig[:, 0, :].unsqueeze(1).to_broadcast([P, heads, HD]),
                op=MULT,
            )
            nc.vector.tensor_tensor(
                out=crossed[:],
                in0=sums.rearrange("p (h f j) -> p h f j", f=2, j=HALF)[:, :, ::-1, :],
                in1=trig[:, 1, :]
                .rearrange("p (f j) -> p f j", j=HALF)
                .unsqueeze(1)
                .to_broadcast([P, heads, 2, HALF]),
                op=MULT,
            )
            adder.tensor_tensor(
                out=result[:],
                in0=straight[:].rearrange("p h d -> p (h d)"),
                in1=crossed[:].rearrange("p h f j -> p (h f j)"),
                op=ADD,
            )
            store(nc.sync, i, first, heads, result)

        def finish(i):
            heads = pieces[i][3] // HD
            if not pieces[i][2]:
                result = work.tile([P, heads * HD], F32, name="result")
                nc.scalar.copy(out=result[:], in_=acc[i][:])
                store(nc.scalar, i, 0, heads, result)
            elif i < last_rotary:
                rotate(i, 0, heads, nc.gpsimd)
            else:
                rotate(i, 0, heads // 2, nc.gpsimd)
                rotate(i, heads // 2, heads - heads // 2, nc.vector)

        regroup(0)
        prepare_x()
        quantise(0)
        regroup(1)
        shuffle_tables()
        regroup(2, [0])
        multiply(0)
        quantise(1)
        regroup(2, [1])
        multiply(1)
        finish(0)
        finish(1)
        regroup(3)
        quantise(2)
        for i in range(n_head, n_pieces):
            if i + 2 < n_pieces:
                regroup(i + 2)
            multiply(i)
            if i + 1 < n_pieces:
                quantise(i + 1)
            finish(i)
